import numpy as np
import ml_dtypes


def mxq(x, axis, fmt="e4m3"):
    dtype, down = {"e4m3": (ml_dtypes.float8_e4m3fn, 7), "e5m2": (ml_dtypes.float8_e5m2, 14)}[fmt]
    v = np.moveaxis(np.asarray(x, np.float32).astype(ml_dtypes.bfloat16).astype(np.float64), axis, -1)
    blocks = v.reshape(v.shape[:-1] + (-1, 32))
    amax = np.abs(blocks).max(-1, keepdims=True)
    byte = np.maximum(np.where(amax > 0, np.frexp(amax)[1] - 1 + 127, 0) - down, 1)
    scale = np.exp2(byte - 127.0)
    codes = (blocks / scale).astype(np.float32).astype(dtype).astype(np.float64)
    return np.moveaxis((codes * scale).reshape(v.shape), -1, axis)


WIDE = False


def mx_kscale(k):
    if not WIDE:
        return np.ones(k)
    levels = np.array([10, -10, 5, -5, 0])
    a = np.random.permutation(np.resize(levels, k // 512 * 4)).reshape(k // 512, 4)
    idx = np.arange(k)
    return np.exp2(a[idx // 512, idx % 128 // 32])


BF16 = ml_dtypes.bfloat16


def bf(x):
    return np.asarray(x, np.float32).astype(BF16)


def f64(x):
    return np.asarray(x).astype(np.float64)


E2M1 = np.array([0.0, 0.5, 1.0, 1.5, 2.0, 3.0, 4.0, 6.0, -0.0, -0.5, -1.0, -1.5, -2.0, -3.0, -4.0, -6.0])


def pack_weight(w, fmt):
    k, n = w.shape
    w = f64(bf(w)).reshape(k // 32, 32, n)
    amax = np.abs(w).max(1)
    if fmt == "e4m3":
        byte = np.frexp(amax)[1] - 1 + 127 - 7
    else:
        mant, ex = np.frexp(amax / 6.0)
        byte = np.where(mant > 0.5, ex, ex - 1) + 127
    byte = np.clip(np.where(amax > 0, byte, 1), 1, 254)
    scaled = (w * np.exp2(127.0 - byte)[:, None, :]).reshape(k, n).astype(np.float32)
    by_word = np.ascontiguousarray(scaled.reshape(k // 512, 128, 4, n).transpose(0, 1, 3, 2))
    if fmt == "e4m3":
        words = by_word.astype(ml_dtypes.float8_e4m3fn).view(np.uint8)
    else:
        c = by_word.astype(ml_dtypes.float4_e2m1fn).view(np.uint8) & 0xF
        words = c[..., 0::2] | (c[..., 1::2] << 4)
    return np.ascontiguousarray(words), np.ascontiguousarray(byte.astype(np.uint8).reshape(k // 512, 16, n))


def unpack_weight(words, scales, fmt):
    g, p, n, _ = words.shape
    if fmt == "e4m3":
        vals = np.ascontiguousarray(words).view(ml_dtypes.float8_e4m3fn).astype(np.float64)
    else:
        nib = np.empty((g, p, n, 4), np.uint8)
        nib[..., 0::2] = words & 0xF
        nib[..., 1::2] = words >> 4
        vals = E2M1[nib]
    vals = vals * np.repeat(np.exp2(scales.astype(np.float64) - 127.0), 8, axis=1)[..., None]
    return vals.transpose(0, 1, 3, 2).reshape(g * 512, n)


N, D, L = 1024, 1024, 4
EPS = 1e-5
SLOPE = 0.1
FMT = "e4m3"


def leaky(v):
    return np.where(v >= 0, v, SLOPE * v)


def layernorm(h, g, b):
    mu = np.mean(h, axis=-1, keepdims=True)
    var = np.mean((h - mu) ** 2, axis=-1, keepdims=True)
    return (h - mu) * (1.0 / np.sqrt(var + EPS)) * g + b


def setup_inputs():
    s, t = mx_kscale(N), mx_kscale(D)
    g = np.random.standard_normal((N, N))
    sq = (g * g.T) ** 2
    lap = 0.5 * (sq / sq.sum(axis=1, keepdims=True) + np.eye(N))
    feat = leaky(np.random.standard_normal((N, D)))
    w = np.random.standard_normal((D, D)) / np.sqrt(D) / t[None, :]
    words, scales = pack_weight(np.ascontiguousarray(w.T), FMT)
    return {"lap": bf(lap * s[None, :]),
            "feat": bf(feat / s[:, None] * t[None, :]),
            "w_words": words,
            "w_scales": scales,
            "gamma": bf(1.0 + 0.1 * np.random.standard_normal(D)),
            "beta": bf(0.1 * np.random.standard_normal(D))}


def reference(lap, feat, w_words, w_scales, gamma, beta):
    m = mxq(f64(lap), 1, "e4m3") @ mxq(f64(feat), 0, "e4m3")
    y = mxq(m, 1, "e4m3") @ unpack_weight(w_words, w_scales, FMT)
    return leaky(layernorm(y, f64(gamma), f64(beta)))

@@ -1,0 +1,264 @@
+from contextlib import ExitStack
+
+import concourse.mybir as mybir
+from concourse.masks import make_identity
+
+FLOPS = 2 * 2 * 1024 * 1024 * 1024
+
+FP8X4 = mybir.dt.float8_e4m3fn_x4
+BF16 = mybir.dt.bfloat16
+F32 = mybir.dt.float32
+I32 = mybir.dt.int32
+U32 = mybir.dt.uint32
+U8 = mybir.dt.uint8
+ACT = mybir.ActivationFunctionType
+ALU = mybir.AluOpType
+
+P = 128
+PACK = 4
+K_PASS = P * PACK
+NODES = 1024
+FEATURES = 1024
+PASSES = NODES // K_PASS
+BLOCKS = NODES // P
+BANK = 512
+HALVES = FEATURES // BANK
+WORDS = K_PASS // 2
+EPS = 1e-5
+SLOPE = 0.1
+
+
+def tile_gcn_pb_kernel(tc, lap, feat, w_words, w_scales, gamma, beta, out):
+    nc = tc.nc
+    with ExitStack() as stack:
+        keep = stack.enter_context(tc.tile_pool(name="keep", bufs=1))
+        stage = stack.enter_context(tc.tile_pool(name="stage", bufs=2))
+        ahead = stack.enter_context(tc.tile_pool(name="ahead", bufs=3))
+        scrap = stack.enter_context(tc.tile_pool(name="scrap", bufs=4))
+        psum_lap = stack.enter_context(tc.psum_pool(name="psum_lap", bufs=2))
+        psum_m = stack.enter_context(tc.psum_pool(name="psum_m", bufs=1))
+        psum_y = stack.enter_context(tc.psum_pool(name="psum_y", bufs=2))
+        stack.enter_context(tc.manual_schedule())
+
+        minus_half = keep.tile([P, 1], F32)
+        nc.gpsimd.memset(minus_half[:], -0.5)
+        identity = keep.tile([P, P], F32)
+        make_identity(nc, identity[:])
+        table_warmer = keep.tile([P, 1], F32)
+        nc.scalar.activation(out=table_warmer[:], in_=minus_half[:], func=ACT.Square)
+        w_planes = keep.tile([P, PASSES, FEATURES], U8, align_bytes=64)
+        nc.vector.memset(w_planes[:].bitcast(I32), 0)
+
+        lap_rows = lap.rearrange("(p b) j -> p b j", b=BLOCKS)
+        out_rows = out.rearrange("(p b) n -> p b n", b=BLOCKS)
+        lap_raw = keep.tile([P, BLOCKS, NODES], BF16)
+        feat_raw = keep.tile([P, PASSES, PACK, FEATURES], BF16)
+        w_codes = keep.tile([P, PASSES, PACK * FEATURES], U8, align_bytes=64)
+        gamma_all = keep.tile([P, FEATURES], BF16)
+        beta_all = keep.tile([P, FEATURES], BF16)
+
+        nc.sync.dma_start(out=lap_raw[:, 0:1, :], in_=lap_rows[:, 0:1, :])
+        for g in range(PASSES):
+            nc.sync.dma_start(
+                out=feat_raw[:, g, :, :],
+                in_=feat[g * K_PASS : (g + 1) * K_PASS, :].rearrange("(p t) f -> p t f", t=PACK),
+            )
+        nc.sync.dma_start(out=lap_raw[:, 1:4, :], in_=lap_rows[:, 1:4, :])
+        for quadrant in range(4):
+            nc.sync.dma_start(
+                out=w_planes[32 * quadrant : 32 * quadrant + 4, :, :].bitcast(I32),
+                in_=w_scales[:, 4 * quadrant : 4 * quadrant + 4, :].rearrange("g r n -> r g n").bitcast(I32),
+            )
+        for g in range(PASSES):
+            nc.sync.dma_start(
+                out=w_codes[:, g, :].bitcast(I32),
+                in_=w_words[g].rearrange("p n t -> p (n t)").bitcast(I32),
+            )
+        nc.sync.dma_start(out=gamma_all[:], in_=gamma.partition_broadcast(P))
+        nc.sync.dma_start(out=beta_all[:], in_=beta.partition_broadcast(P))
+        nc.sync.dma_start(out=lap_raw[:, 4:BLOCKS, :], in_=lap_rows[:, 4:BLOCKS, :])
+
+        lap_mx = {}
+        m_banks = {}
+        m_bf16 = {}
+        m_mx = {}
+        y_banks = {}
+        neg_mean = {}
+        inv_std = {}
+        centred = {}
+
+        def quantise_lap(b):
+            if b not in range(BLOCKS):
+                return
+            words = lap_raw[:, b, :].bitcast(F32)
+            lap_t = psum_lap.tile([P, PASSES, 2, P], F32)
+            for g in range(PASSES):
+                for u in range(2):
+                    nc.tensor.transpose(
+                        lap_t[:, g, u, :], words[:, g * WORDS + u : (g + 1) * WORDS : 2], identity[:]
+                    )
+            lap_grouped = stage.tile([P, PASSES, P, PACK], BF16, align_bytes=64)
+            nc.scalar.copy(out=lap_grouped[:].bitcast(F32), in_=lap_t[:].rearrange("p g u i -> p g i u"))
+            lap_codes = ahead.tile([P, PASSES * P], U32, align_bytes=64)
+            lap_planes = ahead.tile([P, PASSES * P], U8, align_bytes=64)
+            nc.vector.quantize_mx(
+                out=lap_codes[:].bitcast(FP8X4),
+                scales=lap_planes[:],
+                in_=lap_grouped[:].rearrange("p g i t -> p (g i t)"),
+            )
+            lap_mx[b] = (lap_codes, lap_planes)
+
+        def first_product(b):
+            if b not in range(BLOCKS):
+                return
+            lap_codes, lap_planes = lap_mx[b]
+            m_low = psum_m.tile([P, PACK, P], F32)
+            m_high = psum_m.tile([P, PACK, P], F32)
+            m_banks[b] = (m_low, m_high)
+            for G in range(PASSES):
+                for T in range(PACK):
+                    for g in range(PASSES):
+                        rows = slice(g * P, (g + 1) * P)
+                        nc.tensor.matmul_mx(
+                            out=m_banks[b][G][:, T, :],
+                            lhsT=feat_codes[:, g, G, T, :].bitcast(FP8X4),
+                            lhsT_scale=feat_planes[:, g, G, T, :],
+                            rhs=lap_codes[:, rows].bitcast(FP8X4),
+                            rhs_scale=lap_planes[:, rows],
+                            start=(g == 0),
+                            stop=(g == PASSES - 1),
+                        )
+
+        def round_m(b):
+            if b not in range(BLOCKS):
+                return
+            m_grouped = stage.tile([P, PASSES, P, PACK], BF16, align_bytes=64)
+            for G in range(PASSES):
+                nc.scalar.copy(out=m_grouped[:, G, :, :], in_=m_banks[b][G][:].rearrange("p T i -> p i T"))
+            m_bf16[b] = m_grouped
+
+        def quantise_m(b):
+            if b not in range(BLOCKS):
+                return
+            m_codes = stage.tile([P, PASSES * P], U32, align_bytes=64)
+            m_planes = stage.tile([P, PASSES * P], U8, align_bytes=64)
+            nc.vector.quantize_mx(
+                out=m_codes[:].bitcast(FP8X4),
+                scales=m_planes[:],
+                in_=m_bf16[b][:].rearrange("p G i T -> p (G i T)"),
+            )
+            m_mx[b] = (m_codes, m_planes)
+
+        def second_product(b):
+            if b not in range(BLOCKS):
+                return
+            m_codes, m_planes = m_mx[b]
+            y_low = psum_y.tile([P, BANK], F32)
+            y_high = psum_y.tile([P, BANK], F32)
+            y_banks[b] = (y_low, y_high)
+            for h in range(HALVES):
+                for G in range(PASSES):
+                    rows = slice(G * P, (G + 1) * P)
+                    nc.tensor.matmul_mx(
+                        out=y_banks[b][h][:],
+                        lhsT=m_codes[:, rows].bitcast(FP8X4),
+                        lhsT_scale=m_planes[:, rows],
+                        rhs=w_codes[:, G, h * PACK * BANK : (h + 1) * PACK * BANK].bitcast(FP8X4),
+                        rhs_scale=w_planes[:, G, h * BANK : (h + 1) * BANK],
+                        start=(G == 0),
+                        stop=(G == PASSES - 1),
+                    )
+
+        def mean_of_rows(b):
+            if b not in range(BLOCKS):
+                return
+            sums = ahead.tile([P, HALVES], F32)
+            for h in range(HALVES):
+                unread = scrap.tile([P, BANK], BF16)
+                nc.scalar.activation(
+                    out=unread[:], in_=y_banks[b][h][:], func=ACT.Identity,
+                    scale=-1.0 / FEATURES, accum_out=sums[:, h : h + 1],
+                )
+            negative_mean = ahead.tile([P, 1], F32)
+            nc.gpsimd.tensor_tensor(out=negative_mean[:], in0=sums[:, 0:1], in1=sums[:, 1:2], op=ALU.add)
+            neg_mean[b] = negative_mean
+
+        def variance_of_rows(b):
+            if b not in range(BLOCKS):
+                return
+            squares = ahead.tile([P, HALVES], F32)
+            for h in range(HALVES):
+                unread = scrap.tile([P, BANK], BF16)
+                nc.scalar.activation(
+                    out=unread[:], in_=y_banks[b][h][:], func=ACT.Square,
+                    bias=neg_mean[b][:], accum_out=squares[:, h : h + 1],
+                )
+            total = ahead.tile([P, 1], F32)
+            nc.gpsimd.tensor_tensor(out=total[:], in0=squares[:, 0:1], in1=squares[:, 1:2], op=ALU.add)
+            variance = ahead.tile([P, 1], F32)
+            nc.gpsimd.tensor_scalar(
+                out=variance[:], in0=total[:], scalar1=1.0 / FEATURES, scalar2=EPS, op0=ALU.mult, op1=ALU.add
+            )
+            inverse_std = ahead.tile([P, 1], F32)
+            nc.gpsimd.tensor_tensor(out=inverse_std[:], in0=variance[:], in1=minus_half[:], op=ALU.pow)
+            inv_std[b] = inverse_std
+
+        def centre_times_gamma(b):
+            if b not in range(BLOCKS):
+                return
+            scaled = ahead.tile([P, FEATURES], F32)
+            for h in range(HALVES):
+                columns = slice(h * BANK, (h + 1) * BANK)
+                nc.vector.scalar_tensor_tensor(
+                    out=scaled[:, columns], in0=y_banks[b][h][:], scalar=neg_mean[b][:],
+                    in1=gamma_all[:, columns], op0=ALU.add, op1=ALU.mult,
+                )
+            centred[b] = scaled
+
+        def finish(b):
+            if b not in range(BLOCKS):
+                return
+            z = stage.tile([P, FEATURES], F32)
+            nc.vector.scalar_tensor_tensor(
+                out=z[:], in0=centred[b][:], scalar=inv_std[b][:], in1=beta_all[:], op0=ALU.mult, op1=ALU.add
+            )
+            result = ahead.tile([P, FEATURES], F32)
+            nc.vector.scalar_tensor_tensor(
+                out=result[:], in0=z[:], scalar=SLOPE, in1=z[:], op0=ALU.mult, op1=ALU.max
+            )
+            nc.sync.dma_start(out=out_rows[:, b, :], in_=result[:])
+
+        quantise_lap(0)
+
+        feat_grouped = keep.tile([P, PASSES, PASSES, PACK, P, PACK], BF16, align_bytes=64)
+        feat_codes = keep.tile([P, PASSES, PASSES, PACK, P], U32, align_bytes=64)
+        feat_planes = keep.tile([P, PASSES, PASSES, PACK, P], U8, align_bytes=64)
+
+        def sorted_features(g, G):
+            return feat_raw[:, g, :, G * K_PASS : (G + 1) * K_PASS].rearrange("p t (c T) -> p T c t", T=PACK)
+
+        def quantise_feat(g, G):
+            nc.vector.quantize_mx(
+                out=feat_codes[:, g, G, :, :].rearrange("p T c -> p (T c)").bitcast(FP8X4),
+                scales=feat_planes[:, g, G, :, :].rearrange("p T c -> p (T c)"),
+                in_=feat_grouped[:, g, G, :, :, :].rearrange("p T c t -> p (T c t)"),
+            )
+
+        for g in range(PASSES):
+            nc.vector.tensor_copy(out=feat_grouped[:, g, 0, :, :, :], in_=sorted_features(g, 0))
+            nc.scalar.copy(out=feat_grouped[:, g, 1, :, :, :], in_=sorted_features(g, 1))
+            if g > 0:
+                quantise_feat(g - 1, 1)
+            quantise_feat(g, 0)
+        quantise_feat(PASSES - 1, 1)
+
+        for step in range(-2, BLOCKS + 1):
+            mean_of_rows(step)
+            round_m(step + 1)
+            first_product(step + 2)
+            finish(step - 1)
+            quantise_m(step + 1)
+            second_product(step + 1)
+            variance_of_rows(step)
+            centre_times_gamma(step)
+            quantise_lap(step + 3)

@@ -74,20 +74,23 @@ def tile_gcn_pb_kernel(tc, lap, feat, w_words, w_scales, gamma, beta, out):
                 out=w_codes[:, g, :].bitcast(I32),
                 in_=w_words[g].rearrange("p n t -> p (n t)").bitcast(I32),
             )
+        nc.sync.dma_start(out=lap_raw[:, 4:BLOCKS, :], in_=lap_rows[:, 4:BLOCKS, :])
         nc.sync.dma_start(out=gamma_all[:], in_=gamma.partition_broadcast(P))
         nc.sync.dma_start(out=beta_all[:], in_=beta.partition_broadcast(P))
-        nc.sync.dma_start(out=lap_raw[:, 4:BLOCKS, :], in_=lap_rows[:, 4:BLOCKS, :])
 
+        lap_banks = {}
         lap_mx = {}
         m_banks = {}
         m_bf16 = {}
         m_mx = {}
         y_banks = {}
+        low_shares = {}
         neg_mean = {}
         inv_std = {}
         centred = {}
+        normalised = {}
 
-        def quantise_lap(b):
+        def transpose_lap(b):
             if b not in range(BLOCKS):
                 return
             words = lap_raw[:, b, :].bitcast(F32)
@@ -97,8 +100,15 @@ def tile_gcn_pb_kernel(tc, lap, feat, w_words, w_scales, gamma, beta, out):
                     nc.tensor.transpose(
                         lap_t[:, g, u, :], words[:, g * WORDS + u : (g + 1) * WORDS : 2], identity[:]
                     )
+            lap_banks[b] = lap_t
+
+        def quantise_lap(b):
+            if b not in range(BLOCKS):
+                return
             lap_grouped = stage.tile([P, PASSES, P, PACK], BF16, align_bytes=64)
-            nc.scalar.copy(out=lap_grouped[:].bitcast(F32), in_=lap_t[:].rearrange("p g u i -> p g i u"))
+            nc.scalar.copy(
+                out=lap_grouped[:].bitcast(F32), in_=lap_banks[b][:].rearrange("p g u i -> p g i u")
+            )
             lap_codes = ahead.tile([P, PASSES * P], U32, align_bytes=64)
             lap_planes = ahead.tile([P, PASSES * P], U8, align_bytes=64)
             nc.vector.quantize_mx(
@@ -129,19 +139,19 @@ def tile_gcn_pb_kernel(tc, lap, feat, w_words, w_scales, gamma, beta, out):
                             stop=(g == PASSES - 1),
                         )
 
-        def round_m(b):
+        def round_m(b, G):
             if b not in range(BLOCKS):
                 return
-            m_grouped = stage.tile([P, PASSES, P, PACK], BF16, align_bytes=64)
-            for G in range(PASSES):
-                nc.scalar.copy(out=m_grouped[:, G, :, :], in_=m_banks[b][G][:].rearrange("p T i -> p i T"))
-            m_bf16[b] = m_grouped
+            if G == 0:
+                m_grouped = stage.tile([P, PASSES, P, PACK], BF16, align_bytes=64)
+                m_bf16[b] = m_grouped
+            nc.scalar.copy(out=m_bf16[b][:, G, :, :], in_=m_banks[b][G][:].rearrange("p T i -> p i T"))
 
         def quantise_m(b):
             if b not in range(BLOCKS):
                 return
-            m_codes = stage.tile([P, PASSES * P], U32, align_bytes=64)
-            m_planes = stage.tile([P, PASSES * P], U8, align_bytes=64)
+            m_codes = ahead.tile([P, PASSES * P], U32, align_bytes=64)
+            m_planes = ahead.tile([P, PASSES * P], U8, align_bytes=64)
             nc.vector.quantize_mx(
                 out=m_codes[:].bitcast(FP8X4),
                 scales=m_planes[:],
@@ -169,19 +179,24 @@ def tile_gcn_pb_kernel(tc, lap, feat, w_words, w_scales, gamma, beta, out):
                         stop=(G == PASSES - 1),
                     )
 
-        def mean_of_rows(b):
+        def mean_of_rows(b, h):
             if b not in range(BLOCKS):
                 return
-            sums = ahead.tile([P, HALVES], F32)
-            for h in range(HALVES):
-                unread = scrap.tile([P, BANK], BF16)
+            unread = scrap.tile([P, BANK], BF16)
+            if h == 0:
+                low_share = ahead.tile([P, 1], F32)
                 nc.scalar.activation(
-                    out=unread[:], in_=y_banks[b][h][:], func=ACT.Identity,
-                    scale=-1.0 / FEATURES, accum_out=sums[:, h : h + 1],
+                    out=unread[:], in_=y_banks[b][0][:], func=ACT.Identity,
+                    scale=-1.0 / (FEATURES * BANK), accum_out=low_share[:],
                 )
-            negative_mean = ahead.tile([P, 1], F32)
-            nc.gpsimd.tensor_tensor(out=negative_mean[:], in0=sums[:, 0:1], in1=sums[:, 1:2], op=ALU.add)
-            neg_mean[b] = negative_mean
+                low_shares[b] = low_share
+            else:
+                negative_mean = ahead.tile([P, 1], F32)
+                nc.scalar.activation(
+                    out=unread[:], in_=y_banks[b][1][:], func=ACT.Identity,
+                    scale=-1.0 / FEATURES, bias=low_shares[b][:], accum_out=negative_mean[:],
+                )
+                neg_mean[b] = negative_mean
 
         def variance_of_rows(b):
             if b not in range(BLOCKS):
@@ -215,20 +230,28 @@ def tile_gcn_pb_kernel(tc, lap, feat, w_words, w_scales, gamma, beta, out):
                 )
             centred[b] = scaled
 
-        def finish(b):
+        def normalise(b):
             if b not in range(BLOCKS):
                 return
             z = stage.tile([P, FEATURES], F32)
             nc.vector.scalar_tensor_tensor(
                 out=z[:], in0=centred[b][:], scalar=inv_std[b][:], in1=beta_all[:], op0=ALU.mult, op1=ALU.add
             )
+            normalised[b] = z
+
+        def leaky_and_store(b):
+            if b not in range(BLOCKS):
+                return
+            z = normalised[b]
             result = ahead.tile([P, FEATURES], F32)
             nc.vector.scalar_tensor_tensor(
                 out=result[:], in0=z[:], scalar=SLOPE, in1=z[:], op0=ALU.mult, op1=ALU.max
             )
             nc.sync.dma_start(out=out_rows[:, b, :], in_=result[:])
 
+        transpose_lap(0)
         quantise_lap(0)
+        transpose_lap(1)
 
         feat_grouped = keep.tile([P, PASSES, PASSES, PACK, P, PACK], BF16, align_bytes=64)
         feat_codes = keep.tile([P, PASSES, PASSES, PACK, P], U32, align_bytes=64)
@@ -252,13 +275,17 @@ def tile_gcn_pb_kernel(tc, lap, feat, w_words, w_scales, gamma, beta, out):
             quantise_feat(g, 0)
         quantise_feat(PASSES - 1, 1)
 
-        for step in range(-2, BLOCKS + 1):
-            mean_of_rows(step)
-            round_m(step + 1)
-            first_product(step + 2)
-            finish(step - 1)
-            quantise_m(step + 1)
+        for step in range(-3, BLOCKS + 1):
+            mean_of_rows(step, 0)
             second_product(step + 1)
+            round_m(step + 2, 0)
+            mean_of_rows(step, 1)
+            round_m(step + 2, 1)
+            quantise_m(step + 2)
+            first_product(step + 3)
             variance_of_rows(step)
+            normalise(step - 1)
             centre_times_gamma(step)
-            quantise_lap(step + 3)
+            leaky_and_store(step - 1)
+            quantise_lap(step + 4)
+            transpose_lap(step + 5)

@@ -52,18 +52,27 @@ def tile_gcn_pb_kernel(tc, lap, feat, w_words, w_scales, gamma, beta, out):
         lap_rows = lap.rearrange("(p b) j -> p b j", b=BLOCKS)
         out_rows = out.rearrange("(p b) n -> p b n", b=BLOCKS)
         lap_raw = keep.tile([P, BLOCKS, NODES], BF16)
-        feat_raw = keep.tile([P, PASSES, PACK, FEATURES], BF16)
         w_codes = keep.tile([P, PASSES, PACK * FEATURES], U8, align_bytes=64)
         gamma_all = keep.tile([P, FEATURES], BF16)
         beta_all = keep.tile([P, FEATURES], BF16)
+        PIECES = [(G, g) for G in range(PASSES) for g in range(PASSES)]
+        feat_raw = {}
+        for G, g in PIECES:
+            feat_raw[(G, g)] = keep.tile([P, PACK, K_PASS], BF16, name="feat_raw_%d_%d" % (G, g))
 
-        nc.sync.dma_start(out=lap_raw[:, 0:1, :], in_=lap_rows[:, 0:1, :])
-        for g in range(PASSES):
+        def load_lap(first, last):
+            nc.sync.dma_start(out=lap_raw[:, first:last, :], in_=lap_rows[:, first:last, :])
+
+        load_lap(0, 1)
+        for G, g in PIECES:
             nc.sync.dma_start(
-                out=feat_raw[:, g, :, :],
-                in_=feat[g * K_PASS : (g + 1) * K_PASS, :].rearrange("(p t) f -> p t f", t=PACK),
+                out=feat_raw[(G, g)][:],
+                in_=feat[g * K_PASS : (g + 1) * K_PASS, G * K_PASS : (G + 1) * K_PASS].rearrange(
+                    "(p t) f -> p t f", t=PACK
+                ),
             )
-        nc.sync.dma_start(out=lap_raw[:, 1:4, :], in_=lap_rows[:, 1:4, :])
+        load_lap(1, 2)
+        load_lap(2, 3)
         for quadrant in range(4):
             nc.sync.dma_start(
                 out=w_planes[32 * quadrant : 32 * quadrant + 4, :, :].bitcast(I32),
@@ -74,11 +83,14 @@ def tile_gcn_pb_kernel(tc, lap, feat, w_words, w_scales, gamma, beta, out):
                 out=w_codes[:, g, :].bitcast(I32),
                 in_=w_words[g].rearrange("p n t -> p (n t)").bitcast(I32),
             )
-        nc.sync.dma_start(out=lap_raw[:, 4:BLOCKS, :], in_=lap_rows[:, 4:BLOCKS, :])
         nc.sync.dma_start(out=gamma_all[:], in_=gamma.partition_broadcast(P))
         nc.sync.dma_start(out=beta_all[:], in_=beta.partition_broadcast(P))
+        load_lap(3, 4)
+        load_lap(4, 5)
+        load_lap(5, BLOCKS)
 
         lap_banks = {}
+        lap_bf16 = {}
         lap_mx = {}
         m_banks = {}
         m_bf16 = {}
@@ -86,6 +98,7 @@ def tile_gcn_pb_kernel(tc, lap, feat, w_words, w_scales, gamma, beta, out):
         y_banks = {}
         low_shares = {}
         neg_mean = {}
+        mean = {}
         inv_std = {}
         centred = {}
         normalised = {}
@@ -102,82 +115,99 @@ def tile_gcn_pb_kernel(tc, lap, feat, w_words, w_scales, gamma, beta, out):
                     )
             lap_banks[b] = lap_t
 
+        def copy_lap(b, on_vector=False):
+            if b not in range(BLOCKS):
+                return
+            lap_grouped = ahead.tile([P, PASSES, P, PACK], BF16, align_bytes=64)
+            source = lap_banks[b][:].rearrange("p g u i -> p g i u")
+            if on_vector:
+                nc.vector.tensor_copy(out=lap_grouped[:].bitcast(F32), in_=source)
+            else:
+                nc.scalar.copy(out=lap_grouped[:].bitcast(F32), in_=source)
+            lap_bf16[b] = lap_grouped
+
         def quantise_lap(b):
             if b not in range(BLOCKS):
                 return
-            lap_grouped = stage.tile([P, PASSES, P, PACK], BF16, align_bytes=64)
-            nc.scalar.copy(
-                out=lap_grouped[:].bitcast(F32), in_=lap_banks[b][:].rearrange("p g u i -> p g i u")
-            )
             lap_codes = ahead.tile([P, PASSES * P], U32, align_bytes=64)
             lap_planes = ahead.tile([P, PASSES * P], U8, align_bytes=64)
             nc.vector.quantize_mx(
                 out=lap_codes[:].bitcast(FP8X4),
                 scales=lap_planes[:],
-                in_=lap_grouped[:].rearrange("p g i t -> p (g i t)"),
+                in_=lap_bf16[b][:].rearrange("p g i t -> p (g i t)"),
             )
             lap_mx[b] = (lap_codes, lap_planes)
 
-        def first_product(b):
+        def first_product(b, G):
             if b not in range(BLOCKS):
                 return
             lap_codes, lap_planes = lap_mx[b]
-            m_low = psum_m.tile([P, PACK, P], F32)
-            m_high = psum_m.tile([P, PACK, P], F32)
-            m_banks[b] = (m_low, m_high)
-            for G in range(PASSES):
-                for T in range(PACK):
-                    for g in range(PASSES):
-                        rows = slice(g * P, (g + 1) * P)
-                        nc.tensor.matmul_mx(
-                            out=m_banks[b][G][:, T, :],
-                            lhsT=feat_codes[:, g, G, T, :].bitcast(FP8X4),
-                            lhsT_scale=feat_planes[:, g, G, T, :],
-                            rhs=lap_codes[:, rows].bitcast(FP8X4),
-                            rhs_scale=lap_planes[:, rows],
-                            start=(g == 0),
-                            stop=(g == PASSES - 1),
-                        )
+            m_half = psum_m.tile([P, PACK, P], F32, name="m_half_%d" % G)
+            m_banks[(b, G)] = m_half
+            for T in range(PACK):
+                for g in range(PASSES):
+                    rows = slice(g * P, (g + 1) * P)
+                    nc.tensor.matmul_mx(
+                        out=m_half[:, T, :],
+                        lhsT=feat_codes[:, g, G, T, :].bitcast(FP8X4),
+                        lhsT_scale=feat_planes[:, g, G, T, :],
+                        rhs=lap_codes[:, rows].bitcast(FP8X4),
+                        rhs_scale=lap_planes[:, rows],
+                        start=(g == 0),
+                        stop=(g == PASSES - 1),
+                    )
 
-        def round_m(b, G):
+        def round_m(b, G, on_vector=False):
             if b not in range(BLOCKS):
                 return
             if G == 0:
                 m_grouped = stage.tile([P, PASSES, P, PACK], BF16, align_bytes=64)
                 m_bf16[b] = m_grouped
-            nc.scalar.copy(out=m_bf16[b][:, G, :, :], in_=m_banks[b][G][:].rearrange("p T i -> p i T"))
+                m_codes = ahead.tile([P, PASSES * P], U32, align_bytes=64)
+                m_planes = ahead.tile([P, PASSES * P], U8, align_bytes=64)
+                m_mx[b] = (m_codes, m_planes)
+            source = m_banks[(b, G)][:].rearrange("p T i -> p i T")
+            if on_vector:
+                nc.vector.tensor_copy(out=m_bf16[b][:, G, :, :], in_=source)
+            else:
+                nc.scalar.copy(out=m_bf16[b][:, G, :, :], in_=source)
 
-        def quantise_m(b):
+        def quantise_m(b, halves=(0, 1)):
             if b not in range(BLOCKS):
                 return
-            m_codes = ahead.tile([P, PASSES * P], U32, align_bytes=64)
-            m_planes = ahead.tile([P, PASSES * P], U8, align_bytes=64)
+            m_codes, m_planes = m_mx[b]
+            columns = slice(halves[0] * P, (halves[-1] + 1) * P)
             nc.vector.quantize_mx(
-                out=m_codes[:].bitcast(FP8X4),
-                scales=m_planes[:],
-                in_=m_bf16[b][:].rearrange("p G i T -> p (G i T)"),
+                out=m_codes[:, columns].bitcast(FP8X4),
+                scales=m_planes[:, columns],
+                in_=m_bf16[b][:, halves[0] : halves[-1] + 1, :, :].rearrange("p G i T -> p (G i T)"),
             )
-            m_mx[b] = (m_codes, m_planes)
+
+        def second_pass(b, h, G):
+            m_codes, m_planes = m_mx[b]
+            rows = slice(G * P, (G + 1) * P)
+            nc.tensor.matmul_mx(
+                out=y_banks[b][h][:],
+                lhsT=m_codes[:, rows].bitcast(FP8X4),
+                lhsT_scale=m_planes[:, rows],
+                rhs=w_codes[:, G, h * PACK * BANK : (h + 1) * PACK * BANK].bitcast(FP8X4),
+                rhs_scale=w_planes[:, G, h * BANK : (h + 1) * BANK],
+                start=(G == 0),
+                stop=(G == PASSES - 1),
+            )
+
+        def open_y(b):
+            y_low = psum_y.tile([P, BANK], F32)
+            y_high = psum_y.tile([P, BANK], F32)
+            y_banks[b] = (y_low, y_high)
 
         def second_product(b):
             if b not in range(BLOCKS):
                 return
-            m_codes, m_planes = m_mx[b]
-            y_low = psum_y.tile([P, BANK], F32)
-            y_high = psum_y.tile([P, BANK], F32)
-            y_banks[b] = (y_low, y_high)
+            open_y(b)
             for h in range(HALVES):
                 for G in range(PASSES):
-                    rows = slice(G * P, (G + 1) * P)
-                    nc.tensor.matmul_mx(
-                        out=y_banks[b][h][:],
-                        lhsT=m_codes[:, rows].bitcast(FP8X4),
-                        lhsT_scale=m_planes[:, rows],
-                        rhs=w_codes[:, G, h * PACK * BANK : (h + 1) * PACK * BANK].bitcast(FP8X4),
-                        rhs_scale=w_planes[:, G, h * BANK : (h + 1) * BANK],
-                        start=(G == 0),
-                        stop=(G == PASSES - 1),
-                    )
+                    second_pass(b, h, G)
 
         def mean_of_rows(b, h):
             if b not in range(BLOCKS):
@@ -218,17 +248,42 @@ def tile_gcn_pb_kernel(tc, lap, feat, w_words, w_scales, gamma, beta, out):
             nc.gpsimd.tensor_tensor(out=inverse_std[:], in0=variance[:], in1=minus_half[:], op=ALU.pow)
             inv_std[b] = inverse_std
 
-        def centre_times_gamma(b):
+        def statistics_on_vector(b):
+            partial = ahead.tile([P, HALVES, 6], F32)
+            for h in range(HALVES):
+                nc.vector.bn_stats(out=partial[:, h, :], in_=y_banks[b][h][:])
+            mean_var = ahead.tile([P, 2], F32)
+            nc.vector.bn_aggr(out=mean_var[:], in_=partial[:].rearrange("p h s -> p (h s)"))
+            mean[b] = mean_var
+            shifted = ahead.tile([P, 1], F32)
+            nc.gpsimd.tensor_scalar(
+                out=shifted[:], in0=mean_var[:, 1:2], scalar1=1.0, scalar2=EPS, op0=ALU.mult, op1=ALU.add
+            )
+            inverse_std = ahead.tile([P, 1], F32)
+            nc.gpsimd.tensor_tensor(out=inverse_std[:], in0=shifted[:], in1=minus_half[:], op=ALU.pow)
+            inv_std[b] = inverse_std
+
+        def centre_half(b, h):
             if b not in range(BLOCKS):
                 return
-            scaled = ahead.tile([P, FEATURES], F32)
-            for h in range(HALVES):
-                columns = slice(h * BANK, (h + 1) * BANK)
+            if h == 0:
+                scaled = ahead.tile([P, FEATURES], F32)
+                centred[b] = scaled
+            columns = slice(h * BANK, (h + 1) * BANK)
+            if b in mean:
                 nc.vector.scalar_tensor_tensor(
-                    out=scaled[:, columns], in0=y_banks[b][h][:], scalar=neg_mean[b][:],
+                    out=centred[b][:, columns], in0=y_banks[b][h][:], scalar=mean[b][:, 0:1],
+                    in1=gamma_all[:, columns], op0=ALU.subtract, op1=ALU.mult,
+                )
+            else:
+                nc.vector.scalar_tensor_tensor(
+                    out=centred[b][:, columns], in0=y_banks[b][h][:], scalar=neg_mean[b][:],
                     in1=gamma_all[:, columns], op0=ALU.add, op1=ALU.mult,
                 )
-            centred[b] = scaled
+
+        def centre_times_gamma(b):
+            centre_half(b, 0)
+            centre_half(b, 1)
 
         def normalise(b):
             if b not in range(BLOCKS):
@@ -239,53 +294,83 @@ def tile_gcn_pb_kernel(tc, lap, feat, w_words, w_scales, gamma, beta, out):
             )
             normalised[b] = z
 
-        def leaky_and_store(b):
+        def leaky_and_store(b, pieces=1):
             if b not in range(BLOCKS):
                 return
             z = normalised[b]
             result = ahead.tile([P, FEATURES], F32)
-            nc.vector.scalar_tensor_tensor(
-                out=result[:], in0=z[:], scalar=SLOPE, in1=z[:], op0=ALU.mult, op1=ALU.max
-            )
-            nc.sync.dma_start(out=out_rows[:, b, :], in_=result[:])
-
-        transpose_lap(0)
-        quantise_lap(0)
-        transpose_lap(1)
+            width = FEATURES // pieces
+            for piece in range(pieces):
+                columns = slice(piece * width, (piece + 1) * width)
+                nc.vector.scalar_tensor_tensor(
+                    out=result[:, columns], in0=z[:, columns], scalar=SLOPE, in1=z[:, columns],
+                    op0=ALU.mult, op1=ALU.max,
+                )
+                nc.sync.dma_start(out=out_rows[:, b, columns], in_=result[:, columns])
 
         feat_grouped = keep.tile([P, PASSES, PASSES, PACK, P, PACK], BF16, align_bytes=64)
         feat_codes = keep.tile([P, PASSES, PASSES, PACK, P], U32, align_bytes=64)
         feat_planes = keep.tile([P, PASSES, PASSES, PACK, P], U8, align_bytes=64)
 
-        def sorted_features(g, G):
-            return feat_raw[:, g, :, G * K_PASS : (G + 1) * K_PASS].rearrange("p t (c T) -> p T c t", T=PACK)
+        def regroup_feat(G, g):
+            source = feat_raw[(G, g)][:].rearrange("p t (c T) -> p T c t", T=PACK)
+            nc.vector.tensor_copy(out=feat_grouped[:, g, G, 0:2, :, :], in_=source[:, 0:2, :, :])
+            nc.scalar.copy(out=feat_grouped[:, g, G, 2:4, :, :], in_=source[:, 2:4, :, :])
 
-        def quantise_feat(g, G):
+        def quantise_feat(G, g):
             nc.vector.quantize_mx(
                 out=feat_codes[:, g, G, :, :].rearrange("p T c -> p (T c)").bitcast(FP8X4),
                 scales=feat_planes[:, g, G, :, :].rearrange("p T c -> p (T c)"),
                 in_=feat_grouped[:, g, G, :, :, :].rearrange("p T c t -> p (T c t)"),
             )
 
-        for g in range(PASSES):
-            nc.vector.tensor_copy(out=feat_grouped[:, g, 0, :, :, :], in_=sorted_features(g, 0))
-            nc.scalar.copy(out=feat_grouped[:, g, 1, :, :, :], in_=sorted_features(g, 1))
-            if g > 0:
-                quantise_feat(g - 1, 1)
-            quantise_feat(g, 0)
-        quantise_feat(PASSES - 1, 1)
-
-        for step in range(-3, BLOCKS + 1):
-            mean_of_rows(step, 0)
-            second_product(step + 1)
-            round_m(step + 2, 0)
-            mean_of_rows(step, 1)
-            round_m(step + 2, 1)
-            quantise_m(step + 2)
-            first_product(step + 3)
-            variance_of_rows(step)
+        transpose_lap(0)
+        copy_lap(0, on_vector=True)
+        regroup_feat(0, 0)
+        quantise_lap(0)
+        regroup_feat(0, 1)
+        quantise_feat(0, 0)
+        regroup_feat(1, 0)
+        quantise_feat(0, 1)
+        first_product(0, 0)
+        regroup_feat(1, 1)
+        quantise_feat(1, 0)
+        transpose_lap(1)
+        transpose_lap(2)
+        quantise_feat(1, 1)
+        round_m(0, 0)
+        first_product(0, 1)
+        quantise_m(0, (0,))
+        copy_lap(1)
+        open_y(0)
+        second_pass(0, 0, 0)
+        second_pass(0, 1, 0)
+        round_m(0, 1)
+        quantise_lap(1)
+        first_product(1, 0)
+        quantise_m(0, (1,))
+        second_pass(0, 0, 1)
+        second_pass(0, 1, 1)
+        copy_lap(2)
+        first_product(1, 1)
+        transpose_lap(3)
+        quantise_lap(2)
+        for step in range(0, BLOCKS + 1):
+            round_m(step + 1, 0)
+            round_m(step + 1, 1)
+            first_product(step + 2, 0)
+            first_product(step + 2, 1)
+            if step == 0:
+                statistics_on_vector(0)
+            else:
+                mean_of_rows(step, 0)
+                mean_of_rows(step, 1)
+                variance_of_rows(step)
             normalise(step - 1)
+            quantise_m(step + 1)
+            second_product(step + 1)
+            leaky_and_store(step - 1, pieces=(2 if step == BLOCKS else 1))
             centre_times_gamma(step)
-            leaky_and_store(step - 1)
-            quantise_lap(step + 4)
-            transpose_lap(step + 5)
+            copy_lap(step + 3)
+            quantise_lap(step + 3)
+            transpose_lap(step + 4)

@@ -83,10 +83,10 @@ def tile_gcn_pb_kernel(tc, lap, feat, w_words, w_scales, gamma, beta, out):
                 out=w_codes[:, g, :].bitcast(I32),
                 in_=w_words[g].rearrange("p n t -> p (n t)").bitcast(I32),
             )
-        nc.sync.dma_start(out=gamma_all[:], in_=gamma.partition_broadcast(P))
-        nc.sync.dma_start(out=beta_all[:], in_=beta.partition_broadcast(P))
         load_lap(3, 4)
         load_lap(4, 5)
+        nc.sync.dma_start(out=gamma_all[:], in_=gamma.partition_broadcast(P))
+        nc.sync.dma_start(out=beta_all[:], in_=beta.partition_broadcast(P))
         load_lap(5, BLOCKS)
 
         lap_banks = {}

@@ -356,21 +356,31 @@ def tile_gcn_pb_kernel(tc, lap, feat, w_words, w_scales, gamma, beta, out):
         transpose_lap(3)
         quantise_lap(2)
         for step in range(0, BLOCKS + 1):
-            round_m(step + 1, 0)
-            round_m(step + 1, 1)
-            first_product(step + 2, 0)
-            first_product(step + 2, 1)
+            if step + 3 < BLOCKS:
+                round_m(step + 1, 0)
+                first_product(step + 2, 0)
+                if step > 0:
+                    mean_of_rows(step, 0)
+                round_m(step + 1, 1)
+                first_product(step + 2, 1)
+                if step > 0:
+                    mean_of_rows(step, 1)
+                copy_lap(step + 3)
+            else:
+                mean_of_rows(step, 0)
+                round_m(step + 1, 0)
+                first_product(step + 2, 0)
+                mean_of_rows(step, 1)
+                round_m(step + 1, 1)
+                first_product(step + 2, 1)
             if step == 0:
                 statistics_on_vector(0)
             else:
-                mean_of_rows(step, 0)
-                mean_of_rows(step, 1)
                 variance_of_rows(step)
             normalise(step - 1)
             quantise_m(step + 1)
             second_product(step + 1)
             leaky_and_store(step - 1, pieces=(2 if step == BLOCKS else 1))
             centre_times_gamma(step)
-            copy_lap(step + 3)
             quantise_lap(step + 3)
             transpose_lap(step + 4)

@@ -313,9 +313,11 @@ def tile_gcn_pb_kernel(tc, lap, feat, w_words, w_scales, gamma, beta, out):
         feat_planes = keep.tile([P, PASSES, PASSES, PACK, P], U8, align_bytes=64)
 
         def regroup_feat(G, g):
-            source = feat_raw[(G, g)][:].rearrange("p t (c T) -> p T c t", T=PACK)
-            nc.vector.tensor_copy(out=feat_grouped[:, g, G, 0:2, :, :], in_=source[:, 0:2, :, :])
-            nc.scalar.copy(out=feat_grouped[:, g, G, 2:4, :, :], in_=source[:, 2:4, :, :])
+            source = feat_raw[(G, g)][:].rearrange("p t (c T) -> p c t T", T=PACK)
+            target = feat_grouped[:, g, G, :, :, :].rearrange("p T c t -> p c t T")
+            half = P // 2
+            nc.vector.tensor_copy(out=target[:, 0:half, :, :], in_=source[:, 0:half, :, :])
+            nc.scalar.copy(out=target[:, half:P, :, :], in_=source[:, half:P, :, :])
 
         def quantise_feat(G, g):
             nc.vector.quantize_mx(

@@ -40,12 +40,12 @@ def tile_gcn_pb_kernel(tc, lap, feat, w_words, w_scales, gamma, beta, out):
         psum_y = stack.enter_context(tc.psum_pool(name="psum_y", bufs=2))
         stack.enter_context(tc.manual_schedule())
 
-        minus_half = keep.tile([P, 1], F32)
-        nc.gpsimd.memset(minus_half[:], -0.5)
+        one = keep.tile([P, 1], F32)
+        nc.gpsimd.memset(one[:], 1.0)
         identity = keep.tile([P, P], F32)
         make_identity(nc, identity[:])
         table_warmer = keep.tile([P, 1], F32)
-        nc.scalar.activation(out=table_warmer[:], in_=minus_half[:], func=ACT.Square)
+        nc.scalar.activation(out=table_warmer[:], in_=one[:], func=ACT.Abs_reciprocal_sqrt)
         w_planes = keep.tile([P, PASSES, FEATURES], U8, align_bytes=64)
         nc.vector.memset(w_planes[:].bitcast(I32), 0)
 
@@ -100,6 +100,7 @@ def tile_gcn_pb_kernel(tc, lap, feat, w_words, w_scales, gamma, beta, out):
         neg_mean = {}
         mean = {}
         inv_std = {}
+        variance_parts = {}
         centred = {}
         normalised = {}
 
@@ -238,14 +239,22 @@ def tile_gcn_pb_kernel(tc, lap, feat, w_words, w_scales, gamma, beta, out):
                     out=unread[:], in_=y_banks[b][h][:], func=ACT.Square,
                     bias=neg_mean[b][:], accum_out=squares[:, h : h + 1],
                 )
-            total = ahead.tile([P, 1], F32)
-            nc.gpsimd.tensor_tensor(out=total[:], in0=squares[:, 0:1], in1=squares[:, 1:2], op=ALU.add)
-            variance = ahead.tile([P, 1], F32)
-            nc.gpsimd.tensor_scalar(
-                out=variance[:], in0=total[:], scalar1=1.0 / FEATURES, scalar2=EPS, op0=ALU.mult, op1=ALU.add
+            low_share = ahead.tile([P, 1], F32, name="variance_share")
+            nc.scalar.activation(
+                out=low_share[:], in_=squares[:, 0:1], func=ACT.Identity, scale=1.0 / FEATURES, bias=EPS
             )
-            inverse_std = ahead.tile([P, 1], F32)
-            nc.gpsimd.tensor_tensor(out=inverse_std[:], in0=variance[:], in1=minus_half[:], op=ALU.pow)
+            variance_parts[b] = (squares, low_share)
+
+        def inverse_std_of_rows(b):
+            if b not in variance_parts:
+                return
+            squares, low_share = variance_parts[b]
+            inverse_std = ahead.tile([P, 1], F32, name="inverse_std_scalar")
+            nc.scalar.activation(
+                out=inverse_std[:], in_=squares[:, 1:2], func=ACT.Abs_reciprocal_sqrt,
+                scale=(1.0 / FEATURES if low_share is not None else 1.0),
+                bias=(low_share[:] if low_share is not None else EPS),
+            )
             inv_std[b] = inverse_std
 
         def statistics_on_vector(b):
@@ -255,13 +264,7 @@ def tile_gcn_pb_kernel(tc, lap, feat, w_words, w_scales, gamma, beta, out):
             mean_var = ahead.tile([P, 2], F32)
             nc.vector.bn_aggr(out=mean_var[:], in_=partial[:].rearrange("p h s -> p (h s)"))
             mean[b] = mean_var
-            shifted = ahead.tile([P, 1], F32)
-            nc.gpsimd.tensor_scalar(
-                out=shifted[:], in0=mean_var[:, 1:2], scalar1=1.0, scalar2=EPS, op0=ALU.mult, op1=ALU.add
-            )
-            inverse_std = ahead.tile([P, 1], F32)
-            nc.gpsimd.tensor_tensor(out=inverse_std[:], in0=shifted[:], in1=minus_half[:], op=ALU.pow)
-            inv_std[b] = inverse_std
+            variance_parts[b] = (mean_var, None)
 
         def centre_half(b, h):
             if b not in range(BLOCKS):
@@ -361,6 +364,7 @@ def tile_gcn_pb_kernel(tc, lap, feat, w_words, w_scales, gamma, beta, out):
             if step + 3 < BLOCKS:
                 round_m(step + 1, 0)
                 first_product(step + 2, 0)
+                inverse_std_of_rows(step - 1)
                 if step > 0:
                     mean_of_rows(step, 0)
                 round_m(step + 1, 1)
@@ -370,6 +374,7 @@ def tile_gcn_pb_kernel(tc, lap, feat, w_words, w_scales, gamma, beta, out):
                 copy_lap(step + 3)
             else:
                 mean_of_rows(step, 0)
+                inverse_std_of_rows(step - 1)
                 round_m(step + 1, 0)
                 first_product(step + 2, 0)
                 mean_of_rows(step, 1)

@@ -26,6 +26,8 @@ HALVES = FEATURES // BANK
 WORDS = K_PASS // 2
 EPS = 1e-5
 SLOPE = 0.1
+FOLDS = FEATURES // P
+FOLDED = (5, 6, 7)
 
 
 def tile_gcn_pb_kernel(tc, lap, feat, w_words, w_scales, gamma, beta, out):
@@ -35,7 +37,8 @@ def tile_gcn_pb_kernel(tc, lap, feat, w_words, w_scales, gamma, beta, out):
         stage = stack.enter_context(tc.tile_pool(name="stage", bufs=2))
         ahead = stack.enter_context(tc.tile_pool(name="ahead", bufs=3))
         scrap = stack.enter_context(tc.tile_pool(name="scrap", bufs=4))
-        psum_lap = stack.enter_context(tc.psum_pool(name="psum_lap", bufs=2))
+        psum_lap = stack.enter_context(tc.psum_pool(name="psum_lap", bufs=1))
+        psum_sum = stack.enter_context(tc.psum_pool(name="psum_sum", bufs=1))
         psum_m = stack.enter_context(tc.psum_pool(name="psum_m", bufs=1))
         psum_y = stack.enter_context(tc.psum_pool(name="psum_y", bufs=2))
         stack.enter_context(tc.manual_schedule())
@@ -96,6 +99,7 @@ def tile_gcn_pb_kernel(tc, lap, feat, w_words, w_scales, gamma, beta, out):
         m_bf16 = {}
         m_mx = {}
         y_banks = {}
+        folded_sums = {}
         low_shares = {}
         neg_mean = {}
         mean = {}
@@ -202,9 +206,38 @@ def tile_gcn_pb_kernel(tc, lap, feat, w_words, w_scales, gamma, beta, out):
             y_high = psum_y.tile([P, BANK], F32)
             y_banks[b] = (y_low, y_high)
 
+        def folded_pass(b, G):
+            m_codes, m_planes = m_mx[b]
+            if G == 0:
+                folded = psum_sum.tile([P, P], F32)
+                folded_sums[b] = folded
+            rows = slice(G * P, (G + 1) * P)
+            for j in range(FOLDS):
+                nc.tensor.matmul_mx(
+                    out=folded_sums[b][:],
+                    lhsT=m_codes[:, rows].bitcast(FP8X4),
+                    lhsT_scale=m_planes[:, rows],
+                    rhs=w_codes[:, G, j * PACK * P : (j + 1) * PACK * P].bitcast(FP8X4),
+                    rhs_scale=w_planes[:, G, j * P : (j + 1) * P],
+                    start=(G == 0 and j == 0),
+                    stop=(G == PASSES - 1 and j == FOLDS - 1),
+                )
+
+        def mean_of_folded(b):
+            unread = scrap.tile([P, P], BF16)
+            negative_mean = ahead.tile([P, 1], F32)
+            nc.scalar.activation(
+                out=unread[:], in_=folded_sums[b][:], func=ACT.Identity,
+                scale=-1.0 / FEATURES, accum_out=negative_mean[:],
+            )
+            neg_mean[b] = negative_mean
+
         def second_product(b):
             if b not in range(BLOCKS):
                 return
+            if b in FOLDED:
+                for G in range(PASSES):
+                    folded_pass(b, G)
             open_y(b)
             for h in range(HALVES):
                 for G in range(PASSES):
@@ -288,14 +321,18 @@ def tile_gcn_pb_kernel(tc, lap, feat, w_words, w_scales, gamma, beta, out):
             centre_half(b, 0)
             centre_half(b, 1)
 
-        def normalise(b):
+        def normalise(b, pieces=1):
             if b not in range(BLOCKS):
                 return
             z = stage.tile([P, FEATURES], F32)
-            nc.vector.scalar_tensor_tensor(
-                out=z[:], in0=centred[b][:], scalar=inv_std[b][:], in1=beta_all[:], op0=ALU.mult, op1=ALU.add
-            )
             normalised[b] = z
+            width = FEATURES // pieces
+            for piece in range(pieces):
+                columns = slice(piece * width, (piece + 1) * width)
+                nc.vector.scalar_tensor_tensor(
+                    out=z[:, columns], in0=centred[b][:, columns], scalar=inv_std[b][:], in1=beta_all[:, columns],
+                    op0=ALU.mult, op1=ALU.add,
+                )
 
         def leaky_and_store(b, pieces=1):
             if b not in range(BLOCKS):
@@ -361,7 +398,15 @@ def tile_gcn_pb_kernel(tc, lap, feat, w_words, w_scales, gamma, beta, out):
         transpose_lap(3)
         quantise_lap(2)
         for step in range(0, BLOCKS + 1):
-            if step + 3 < BLOCKS:
+            if step in FOLDED:
+                round_m(step + 1, 0)
+                first_product(step + 2, 0)
+                inverse_std_of_rows(step - 1)
+                round_m(step + 1, 1)
+                first_product(step + 2, 1)
+                mean_of_folded(step)
+                copy_lap(step + 3)
+            elif step + 3 < BLOCKS:
                 round_m(step + 1, 0)
                 first_product(step + 2, 0)
                 inverse_std_of_rows(step - 1)
@@ -384,10 +429,15 @@ def tile_gcn_pb_kernel(tc, lap, feat, w_words, w_scales, gamma, beta, out):
                 statistics_on_vector(0)
             else:
                 variance_of_rows(step)
-            normalise(step - 1)
+            last_pieces = 2 if step == BLOCKS else 1
+            normalise(step - 1, last_pieces)
             quantise_m(step + 1)
             second_product(step + 1)
-            leaky_and_store(step - 1, pieces=(2 if step == BLOCKS else 1))
-            centre_times_gamma(step)
-            quantise_lap(step + 3)
+            if step + 3 < BLOCKS:
+                leaky_and_store(step - 1)
+                centre_times_gamma(step)
+                quantise_lap(step + 3)
+            else:
+                centre_times_gamma(step)
+                leaky_and_store(step - 1, last_pieces)
             transpose_lap(step + 4)

@@ -37,8 +37,7 @@ def tile_gcn_pb_kernel(tc, lap, feat, w_words, w_scales, gamma, beta, out):
         stage = stack.enter_context(tc.tile_pool(name="stage", bufs=2))
         ahead = stack.enter_context(tc.tile_pool(name="ahead", bufs=3))
         scrap = stack.enter_context(tc.tile_pool(name="scrap", bufs=4))
-        psum_lap = stack.enter_context(tc.psum_pool(name="psum_lap", bufs=1))
-        psum_sum = stack.enter_context(tc.psum_pool(name="psum_sum", bufs=1))
+        psum_lap = stack.enter_context(tc.psum_pool(name="psum_lap", bufs=2))
         psum_m = stack.enter_context(tc.psum_pool(name="psum_m", bufs=1))
         psum_y = stack.enter_context(tc.psum_pool(name="psum_y", bufs=2))
         stack.enter_context(tc.manual_schedule())
@@ -112,7 +111,7 @@ def tile_gcn_pb_kernel(tc, lap, feat, w_words, w_scales, gamma, beta, out):
             if b not in range(BLOCKS):
                 return
             words = lap_raw[:, b, :].bitcast(F32)
-            lap_t = psum_lap.tile([P, PASSES, 2, P], F32)
+            lap_t = psum_lap.tile([P, PASSES, 2, P], F32, name="lap_t")
             for g in range(PASSES):
                 for u in range(2):
                     nc.tensor.transpose(
@@ -209,7 +208,7 @@ def tile_gcn_pb_kernel(tc, lap, feat, w_words, w_scales, gamma, beta, out):
         def folded_pass(b, G):
             m_codes, m_planes = m_mx[b]
             if G == 0:
-                folded = psum_sum.tile([P, P], F32)
+                folded = psum_lap.tile([P, P], F32, name="lap_t")
                 folded_sums[b] = folded
             rows = slice(G * P, (G + 1) * P)
             for j in range(FOLDS):
@@ -391,13 +390,24 @@ def tile_gcn_pb_kernel(tc, lap, feat, w_words, w_scales, gamma, beta, out):
         quantise_lap(1)
         first_product(1, 0)
         quantise_m(0, (1,))
+        first_product(1, 1)
         second_pass(0, 0, 1)
         second_pass(0, 1, 1)
         copy_lap(2)
-        first_product(1, 1)
-        transpose_lap(3)
         quantise_lap(2)
-        for step in range(0, BLOCKS + 1):
+        round_m(1, 0)
+        first_product(2, 0)
+        round_m(1, 1)
+        transpose_lap(3)
+        first_product(2, 1)
+        copy_lap(3)
+        statistics_on_vector(0)
+        quantise_m(1)
+        second_product(1)
+        centre_times_gamma(0)
+        quantise_lap(3)
+        transpose_lap(4)
+        for step in range(1, BLOCKS + 1):
             if step in FOLDED:
                 round_m(step + 1, 0)
                 first_product(step + 2, 0)
@@ -410,12 +420,10 @@ def tile_gcn_pb_kernel(tc, lap, feat, w_words, w_scales, gamma, beta, out):
                 round_m(step + 1, 0)
                 first_product(step + 2, 0)
                 inverse_std_of_rows(step - 1)
-                if step > 0:
-                    mean_of_rows(step, 0)
+                mean_of_rows(step, 0)
                 round_m(step + 1, 1)
                 first_product(step + 2, 1)
-                if step > 0:
-                    mean_of_rows(step, 1)
+                mean_of_rows(step, 1)
                 copy_lap(step + 3)
             else:
                 mean_of_rows(step, 0)
@@ -425,10 +433,7 @@ def tile_gcn_pb_kernel(tc, lap, feat, w_words, w_scales, gamma, beta, out):
                 mean_of_rows(step, 1)
                 round_m(step + 1, 1)
                 first_product(step + 2, 1)
-            if step == 0:
-                statistics_on_vector(0)
-            else:
-                variance_of_rows(step)
+            variance_of_rows(step)
             last_pieces = 2 if step == BLOCKS else 1
             normalise(step - 1, last_pieces)
             quantise_m(step + 1)

@@ -28,6 +28,7 @@ EPS = 1e-5
 SLOPE = 0.1
 FOLDS = FEATURES // P
 FOLDED = (5, 6, 7)
+SHARED_FROM = 512
 
 
 def tile_gcn_pb_kernel(tc, lap, feat, w_words, w_scales, gamma, beta, out):
@@ -37,7 +38,7 @@ def tile_gcn_pb_kernel(tc, lap, feat, w_words, w_scales, gamma, beta, out):
         stage = stack.enter_context(tc.tile_pool(name="stage", bufs=2))
         ahead = stack.enter_context(tc.tile_pool(name="ahead", bufs=3))
         scrap = stack.enter_context(tc.tile_pool(name="scrap", bufs=4))
-        psum_lap = stack.enter_context(tc.psum_pool(name="psum_lap", bufs=2))
+        psum_lap = stack.enter_context(tc.psum_pool(name="psum_lap", bufs=1))
         psum_m = stack.enter_context(tc.psum_pool(name="psum_m", bufs=1))
         psum_y = stack.enter_context(tc.psum_pool(name="psum_y", bufs=2))
         stack.enter_context(tc.manual_schedule())
@@ -46,6 +47,8 @@ def tile_gcn_pb_kernel(tc, lap, feat, w_words, w_scales, gamma, beta, out):
         nc.gpsimd.memset(one[:], 1.0)
         identity = keep.tile([P, P], F32)
         make_identity(nc, identity[:])
+        identity_bf16 = keep.tile([P, P], BF16)
+        nc.gpsimd.tensor_copy(out=identity_bf16[:], in_=identity[:])
         table_warmer = keep.tile([P, 1], F32)
         nc.scalar.activation(out=table_warmer[:], in_=one[:], func=ACT.Abs_reciprocal_sqrt)
         w_planes = keep.tile([P, PASSES, FEATURES], U8, align_bytes=64)
@@ -99,6 +102,7 @@ def tile_gcn_pb_kernel(tc, lap, feat, w_words, w_scales, gamma, beta, out):
         m_mx = {}
         y_banks = {}
         folded_sums = {}
+        negative_parts = {}
         low_shares = {}
         neg_mean = {}
         mean = {}
@@ -111,7 +115,7 @@ def tile_gcn_pb_kernel(tc, lap, feat, w_words, w_scales, gamma, beta, out):
             if b not in range(BLOCKS):
                 return
             words = lap_raw[:, b, :].bitcast(F32)
-            lap_t = psum_lap.tile([P, PASSES, 2, P], F32, name="lap_t")
+            lap_t = psum_lap.tile([P, PASSES, 2, P], F32, name="lap_t_%d" % (b % 2))
             for g in range(PASSES):
                 for u in range(2):
                     nc.tensor.transpose(
@@ -208,7 +212,7 @@ def tile_gcn_pb_kernel(tc, lap, feat, w_words, w_scales, gamma, beta, out):
         def folded_pass(b, G):
             m_codes, m_planes = m_mx[b]
             if G == 0:
-                folded = psum_lap.tile([P, P], F32, name="lap_t")
+                folded = psum_lap.tile([P, P], F32, name="lap_t_1")
                 folded_sums[b] = folded
             rows = slice(G * P, (G + 1) * P)
             for j in range(FOLDS):
@@ -320,6 +324,18 @@ def tile_gcn_pb_kernel(tc, lap, feat, w_words, w_scales, gamma, beta, out):
             centre_half(b, 0)
             centre_half(b, 1)
 
+        beta_source = [beta_all]
+        beta_banks = []
+
+        def beta_to_psum():
+            bank = psum_lap.tile([P, FEATURES], BF16, name="lap_t_0")
+            for h in range(HALVES):
+                columns = slice(h * BANK, (h + 1) * BANK)
+                nc.tensor.matmul(
+                    out=bank[:, columns], lhsT=identity_bf16[:], rhs=beta_all[:, columns], start=True, stop=True
+                )
+            beta_banks.append(bank)
+
         def normalise(b, pieces=1):
             if b not in range(BLOCKS):
                 return
@@ -329,15 +345,35 @@ def tile_gcn_pb_kernel(tc, lap, feat, w_words, w_scales, gamma, beta, out):
             for piece in range(pieces):
                 columns = slice(piece * width, (piece + 1) * width)
                 nc.vector.scalar_tensor_tensor(
-                    out=z[:, columns], in0=centred[b][:, columns], scalar=inv_std[b][:], in1=beta_all[:, columns],
+                    out=z[:, columns], in0=centred[b][:, columns], scalar=inv_std[b][:], in1=beta_source[0][:, columns],
                     op0=ALU.mult, op1=ALU.add,
                 )
+
+        def negative_part(b):
+            part = ahead.tile([P, FEATURES - SHARED_FROM], F32)
+            nc.scalar.activation(
+                out=part[:], in_=normalised[b][:, SHARED_FROM:], func=ACT.Relu, scale=SLOPE - 1.0
+            )
+            negative_parts[b] = part
+
+        def leaky_shared(b):
+            z = normalised[b]
+            result = ahead.tile([P, FEATURES], F32, name="result")
+            nc.gpsimd.tensor_tensor(
+                out=result[:, SHARED_FROM:], in0=z[:, SHARED_FROM:], in1=negative_parts[b][:], op=ALU.add
+            )
+            nc.vector.scalar_tensor_tensor(
+                out=result[:, 0:SHARED_FROM], in0=z[:, 0:SHARED_FROM], scalar=SLOPE, in1=z[:, 0:SHARED_FROM],
+                op0=ALU.mult, op1=ALU.max,
+            )
+            for columns in (slice(0, SHARED_FROM), slice(SHARED_FROM, FEATURES)):
+                nc.sync.dma_start(out=out_rows[:, b, columns], in_=result[:, columns])
 
         def leaky_and_store(b, pieces=1):
             if b not in range(BLOCKS):
                 return
             z = normalised[b]
-            result = ahead.tile([P, FEATURES], F32)
+            result = ahead.tile([P, FEATURES], F32, name="result")
             width = FEATURES // pieces
             for piece in range(pieces):
                 columns = slice(piece * width, (piece + 1) * width)
@@ -408,12 +444,16 @@ def tile_gcn_pb_kernel(tc, lap, feat, w_words, w_scales, gamma, beta, out):
         quantise_lap(3)
         transpose_lap(4)
         for step in range(1, BLOCKS + 1):
+            late = step + 3 >= BLOCKS
+            shared = late and step < BLOCKS
             if step in FOLDED:
                 round_m(step + 1, 0)
                 first_product(step + 2, 0)
                 inverse_std_of_rows(step - 1)
                 round_m(step + 1, 1)
                 first_product(step + 2, 1)
+                if shared:
+                    normalise(step - 1)
                 mean_of_folded(step)
                 copy_lap(step + 3)
             elif step + 3 < BLOCKS:
@@ -423,26 +463,28 @@ def tile_gcn_pb_kernel(tc, lap, feat, w_words, w_scales, gamma, beta, out):
                 mean_of_rows(step, 0)
                 round_m(step + 1, 1)
                 first_product(step + 2, 1)
+                if step + 4 == BLOCKS:
+                    beta_to_psum()
                 mean_of_rows(step, 1)
                 copy_lap(step + 3)
             else:
-                mean_of_rows(step, 0)
                 inverse_std_of_rows(step - 1)
-                round_m(step + 1, 0)
-                first_product(step + 2, 0)
-                mean_of_rows(step, 1)
-                round_m(step + 1, 1)
-                first_product(step + 2, 1)
             variance_of_rows(step)
-            last_pieces = 2 if step == BLOCKS else 1
-            normalise(step - 1, last_pieces)
+            if shared:
+                negative_part(step - 1)
+            if not shared:
+                normalise(step - 1, 2 if step == BLOCKS else 1)
             quantise_m(step + 1)
             second_product(step + 1)
-            if step + 3 < BLOCKS:
+            if not late:
                 leaky_and_store(step - 1)
                 centre_times_gamma(step)
                 quantise_lap(step + 3)
-            else:
+            elif shared:
+                leaky_shared(step - 1)
                 centre_times_gamma(step)
-                leaky_and_store(step - 1, last_pieces)
+            else:
+                leaky_and_store(step - 1, 2)
             transpose_lap(step + 4)
+            if step + 4 == BLOCKS:
+                beta_source[0] = beta_banks[0]

@@ -205,8 +205,8 @@ def tile_gcn_pb_kernel(tc, lap, feat, w_words, w_scales, gamma, beta, out):
             )
 
         def open_y(b):
-            y_low = psum_y.tile([P, BANK], F32)
-            y_high = psum_y.tile([P, BANK], F32)
+            y_low = psum_y.tile([P, BANK], F32, name="y_low")
+            y_high = psum_y.tile([P, BANK], F32, name="y_high")
             y_banks[b] = (y_low, y_high)
 
         def folded_pass(b, G):
@@ -401,14 +401,25 @@ def tile_gcn_pb_kernel(tc, lap, feat, w_words, w_scales, gamma, beta, out):
                 in_=feat_grouped[:, g, G, :, :, :].rearrange("p T c t -> p (T c t)"),
             )
 
+        def keep_tensor_awake(G, g):
+            for bank in ("y_low", "y_high"):
+                unread_bank = psum_y.tile([P, BANK], F32, name=bank)
+                nc.tensor.matmul(
+                    out=unread_bank[:], lhsT=identity_bf16[:], rhs=feat_raw[(G, g)][:, 0, :], start=True, stop=True
+                )
+
         transpose_lap(0)
         copy_lap(0, on_vector=True)
+        keep_tensor_awake(0, 0)
         regroup_feat(0, 0)
         quantise_lap(0)
+        keep_tensor_awake(0, 1)
         regroup_feat(0, 1)
         quantise_feat(0, 0)
+        keep_tensor_awake(1, 0)
         regroup_feat(1, 0)
         quantise_feat(0, 1)
+        keep_tensor_awake(1, 1)
         first_product(0, 0)
         regroup_feat(1, 1)
         quantise_feat(1, 0)

@@ -27,7 +27,7 @@ WORDS = K_PASS // 2
 EPS = 1e-5
 SLOPE = 0.1
 FOLDS = FEATURES // P
-FOLDED = (5, 6, 7)
+FOLDED = (3, 5, 6, 7)
 SHARED_FROM = 512
 
 
@@ -293,10 +293,16 @@ def tile_gcn_pb_kernel(tc, lap, feat, w_words, w_scales, gamma, beta, out):
             )
             inv_std[b] = inverse_std
 
-        def statistics_on_vector(b):
+        bank_statistics = {}
+
+        def statistics_of_banks(b):
             partial = ahead.tile([P, HALVES, 6], F32)
             for h in range(HALVES):
                 nc.vector.bn_stats(out=partial[:, h, :], in_=y_banks[b][h][:])
+            bank_statistics[b] = partial
+
+        def statistics_of_rows(b):
+            partial = bank_statistics[b]
             mean_var = ahead.tile([P, 2], F32)
             nc.vector.bn_aggr(out=mean_var[:], in_=partial[:].rearrange("p h s -> p (h s)"))
             mean[b] = mean_var
@@ -401,25 +407,14 @@ def tile_gcn_pb_kernel(tc, lap, feat, w_words, w_scales, gamma, beta, out):
                 in_=feat_grouped[:, g, G, :, :, :].rearrange("p T c t -> p (T c t)"),
             )
 
-        def keep_tensor_awake(G, g):
-            for bank in ("y_low", "y_high"):
-                unread_bank = psum_y.tile([P, BANK], F32, name=bank)
-                nc.tensor.matmul(
-                    out=unread_bank[:], lhsT=identity_bf16[:], rhs=feat_raw[(G, g)][:, 0, :], start=True, stop=True
-                )
-
         transpose_lap(0)
         copy_lap(0, on_vector=True)
-        keep_tensor_awake(0, 0)
         regroup_feat(0, 0)
         quantise_lap(0)
-        keep_tensor_awake(0, 1)
         regroup_feat(0, 1)
         quantise_feat(0, 0)
-        keep_tensor_awake(1, 0)
         regroup_feat(1, 0)
         quantise_feat(0, 1)
-        keep_tensor_awake(1, 1)
         first_product(0, 0)
         regroup_feat(1, 1)
         quantise_feat(1, 0)
@@ -448,8 +443,9 @@ def tile_gcn_pb_kernel(tc, lap, feat, w_words, w_scales, gamma, beta, out):
         transpose_lap(3)
         first_product(2, 1)
         copy_lap(3)
-        statistics_on_vector(0)
+        statistics_of_banks(0)
         quantise_m(1)
+        statistics_of_rows(0)
         second_product(1)
         centre_times_gamma(0)
         quantise_lap(3)
@@ -460,11 +456,12 @@ def tile_gcn_pb_kernel(tc, lap, feat, w_words, w_scales, gamma, beta, out):
             if step in FOLDED:
                 round_m(step + 1, 0)
                 first_product(step + 2, 0)
-                inverse_std_of_rows(step - 1)
+                if step + 3 <= BLOCKS:
+                    inverse_std_of_rows(step - 1)
                 round_m(step + 1, 1)
                 first_product(step + 2, 1)
                 if shared:
-                    normalise(step - 1)
+                    normalise(step - 1, 2)
                 mean_of_folded(step)
                 copy_lap(step + 3)
             elif step + 3 < BLOCKS:
@@ -478,13 +475,14 @@ def tile_gcn_pb_kernel(tc, lap, feat, w_words, w_scales, gamma, beta, out):
                     beta_to_psum()
                 mean_of_rows(step, 1)
                 copy_lap(step + 3)
-            else:
-                inverse_std_of_rows(step - 1)
             variance_of_rows(step)
             if shared:
                 negative_part(step - 1)
+                inverse_std_of_rows(step)
             if not shared:
                 normalise(step - 1, 2 if step == BLOCKS else 1)
+            if step + 1 in FOLDED:
+                transpose_lap(step + 4)
             quantise_m(step + 1)
             second_product(step + 1)
             if not late:
@@ -495,7 +493,8 @@ def tile_gcn_pb_kernel(tc, lap, feat, w_words, w_scales, gamma, beta, out):
                 leaky_shared(step - 1)
                 centre_times_gamma(step)
             else:
-                leaky_and_store(step - 1, 2)
-            transpose_lap(step + 4)
+                leaky_and_store(step - 1, 4)
+            if not (step + 1 in FOLDED):
+                transpose_lap(step + 4)
             if step + 4 == BLOCKS:
                 beta_source[0] = beta_banks[0]

@@ -396,7 +396,7 @@ def tile_gcn_pb_kernel(tc, lap, feat, w_words, w_scales, gamma, beta, out):
         def regroup_feat(G, g):
             source = feat_raw[(G, g)][:].rearrange("p t (c T) -> p c t T", T=PACK)
             target = feat_grouped[:, g, G, :, :, :].rearrange("p T c t -> p c t T")
-            half = P // 2
+            half = 72
             nc.vector.tensor_copy(out=target[:, 0:half, :, :], in_=source[:, 0:half, :, :])
             nc.scalar.copy(out=target[:, half:P, :, :], in_=source[:, half:P, :, :])
 
@@ -408,7 +408,7 @@ def tile_gcn_pb_kernel(tc, lap, feat, w_words, w_scales, gamma, beta, out):
             )
 
         transpose_lap(0)
-        copy_lap(0, on_vector=True)
+        copy_lap(0)
         regroup_feat(0, 0)
         quantise_lap(0)
         regroup_feat(0, 1)

from contextlib import ExitStack

import concourse.mybir as mybir
from concourse.masks import make_identity

FLOPS = 2 * 2 * 1024 * 1024 * 1024

FP8X4 = mybir.dt.float8_e4m3fn_x4
BF16 = mybir.dt.bfloat16
F32 = mybir.dt.float32
I32 = mybir.dt.int32
U32 = mybir.dt.uint32
U8 = mybir.dt.uint8
ACT = mybir.ActivationFunctionType
ALU = mybir.AluOpType

P = 128
PACK = 4
K_PASS = P * PACK
NODES = 1024
FEATURES = 1024
PASSES = NODES // K_PASS
BLOCKS = NODES // P
BANK = 512
HALVES = FEATURES // BANK
WORDS = K_PASS // 2
EPS = 1e-5
SLOPE = 0.1
FOLDS = FEATURES // P
FOLDED = (3, 5, 6, 7)
SHARED_FROM = 512


def tile_gcn_pb_kernel(tc, lap, feat, w_words, w_scales, gamma, beta, out):
    nc = tc.nc
    with ExitStack() as stack:
        keep = stack.enter_context(tc.tile_pool(name="keep", bufs=1))
        stage = stack.enter_context(tc.tile_pool(name="stage", bufs=2))
        ahead = stack.enter_context(tc.tile_pool(name="ahead", bufs=3))
        scrap = stack.enter_context(tc.tile_pool(name="scrap", bufs=4))
        psum_lap = stack.enter_context(tc.psum_pool(name="psum_lap", bufs=1))
        psum_m = stack.enter_context(tc.psum_pool(name="psum_m", bufs=1))
        psum_y = stack.enter_context(tc.psum_pool(name="psum_y", bufs=2))
        stack.enter_context(tc.manual_schedule())

        one = keep.tile([P, 1], F32)
        nc.gpsimd.memset(one[:], 1.0)
        identity = keep.tile([P, P], F32)
        make_identity(nc, identity[:])
        identity_bf16 = keep.tile([P, P], BF16)
        nc.gpsimd.tensor_copy(out=identity_bf16[:], in_=identity[:])
        table_warmer = keep.tile([P, 1], F32)
        nc.scalar.activation(out=table_warmer[:], in_=one[:], func=ACT.Abs_reciprocal_sqrt)
        w_planes = keep.tile([P, PASSES, FEATURES], U8, align_bytes=64)
        nc.vector.memset(w_planes[:].bitcast(I32), 0)

        lap_rows = lap.rearrange("(p b) j -> p b j", b=BLOCKS)
        out_rows = out.rearrange("(p b) n -> p b n", b=BLOCKS)
        lap_raw = keep.tile([P, BLOCKS, NODES], BF16)
        w_codes = keep.tile([P, PASSES, PACK * FEATURES], U8, align_bytes=64)
        gamma_all = keep.tile([P, FEATURES], BF16)
        beta_all = keep.tile([P, FEATURES], BF16)
        PIECES = [(G, g) for G in range(PASSES) for g in range(PASSES)]
        feat_raw = {}
        for G, g in PIECES:
            feat_raw[(G, g)] = keep.tile([P, PACK, K_PASS], BF16, name="feat_raw_%d_%d" % (G, g))

        def load_lap(first, last):
            nc.sync.dma_start(out=lap_raw[:, first:last, :], in_=lap_rows[:, first:last, :])

        load_lap(0, 1)
        for G, g in PIECES:
            nc.sync.dma_start(
                out=feat_raw[(G, g)][:],
                in_=feat[g * K_PASS : (g + 1) * K_PASS, G * K_PASS : (G + 1) * K_PASS].rearrange(
                    "(p t) f -> p t f", t=PACK
                ),
            )
        load_lap(1, 2)
        load_lap(2, 3)
        for quadrant in range(4):
            nc.sync.dma_start(
                out=w_planes[32 * quadrant : 32 * quadrant + 4, :, :].bitcast(I32),
                in_=w_scales[:, 4 * quadrant : 4 * quadrant + 4, :].rearrange("g r n -> r g n").bitcast(I32),
            )
        for g in range(PASSES):
            nc.sync.dma_start(
                out=w_codes[:, g, :].bitcast(I32),
                in_=w_words[g].rearrange("p n t -> p (n t)").bitcast(I32),
            )
        load_lap(3, 4)
        load_lap(4, 5)
        nc.sync.dma_start(out=gamma_all[:], in_=gamma.partition_broadcast(P))
        nc.sync.dma_start(out=beta_all[:], in_=beta.partition_broadcast(P))
        load_lap(5, BLOCKS)

        lap_banks = {}
        lap_bf16 = {}
        lap_mx = {}
        m_banks = {}
        m_bf16 = {}
        m_mx = {}
        y_banks = {}
        folded_sums = {}
        negative_parts = {}
        low_shares = {}
        neg_mean = {}
        mean = {}
        inv_std = {}
        variance_parts = {}
        centred = {}
        normalised = {}

        def transpose_lap(b):
            if b not in range(BLOCKS):
                return
            words = lap_raw[:, b, :].bitcast(F32)
            lap_t = psum_lap.tile([P, PASSES, 2, P], F32, name="lap_t_%d" % (b % 2))
            for g in range(PASSES):
                for u in range(2):
                    nc.tensor.transpose(
                        lap_t[:, g, u, :], words[:, g * WORDS + u : (g + 1) * WORDS : 2], identity[:]
                    )
            lap_banks[b] = lap_t

        def copy_lap(b, on_vector=False):
            if b not in range(BLOCKS):
                return
            lap_grouped = ahead.tile([P, PASSES, P, PACK], BF16, align_bytes=64)
            source = lap_banks[b][:].rearrange("p g u i -> p g i u")
            if on_vector:
                nc.vector.tensor_copy(out=lap_grouped[:].bitcast(F32), in_=source)
            else:
                nc.scalar.copy(out=lap_grouped[:].bitcast(F32), in_=source)
            lap_bf16[b] = lap_grouped

        def quantise_lap(b):
            if b not in range(BLOCKS):
                return
            lap_codes = ahead.tile([P, PASSES * P], U32, align_bytes=64)
            lap_planes = ahead.tile([P, PASSES * P], U8, align_bytes=64)
            nc.vector.quantize_mx(
                out=lap_codes[:].bitcast(FP8X4),
                scales=lap_planes[:],
                in_=lap_bf16[b][:].rearrange("p g i t -> p (g i t)"),
            )
            lap_mx[b] = (lap_codes, lap_planes)

        def first_product(b, G):
            if b not in range(BLOCKS):
                return
            lap_codes, lap_planes = lap_mx[b]
            m_half = psum_m.tile([P, PACK, P], F32, name="m_half_%d" % G)
            m_banks[(b, G)] = m_half
            for T in range(PACK):
                for g in range(PASSES):
                    rows = slice(g * P, (g + 1) * P)
                    nc.tensor.matmul_mx(
                        out=m_half[:, T, :],
                        lhsT=feat_codes[:, g, G, T, :].bitcast(FP8X4),
                        lhsT_scale=feat_planes[:, g, G, T, :],
                        rhs=lap_codes[:, rows].bitcast(FP8X4),
                        rhs_scale=lap_planes[:, rows],
                        start=(g == 0),
                        stop=(g == PASSES - 1),
                    )

        def round_m(b, G, on_vector=False):
            if b not in range(BLOCKS):
                return
            if G == 0:
                m_grouped = stage.tile([P, PASSES, P, PACK], BF16, align_bytes=64)
                m_bf16[b] = m_grouped
                m_codes = ahead.tile([P, PASSES * P], U32, align_bytes=64)
                m_planes = ahead.tile([P, PASSES * P], U8, align_bytes=64)
                m_mx[b] = (m_codes, m_planes)
            source = m_banks[(b, G)][:].rearrange("p T i -> p i T")
            if on_vector:
                nc.vector.tensor_copy(out=m_bf16[b][:, G, :, :], in_=source)
            else:
                nc.scalar.copy(out=m_bf16[b][:, G, :, :], in_=source)

        def quantise_m(b, halves=(0, 1)):
            if b not in range(BLOCKS):
                return
            m_codes, m_planes = m_mx[b]
            columns = slice(halves[0] * P, (halves[-1] + 1) * P)
            nc.vector.quantize_mx(
                out=m_codes[:, columns].bitcast(FP8X4),
                scales=m_planes[:, columns],
                in_=m_bf16[b][:, halves[0] : halves[-1] + 1, :, :].rearrange("p G i T -> p (G i T)"),
            )

        def second_pass(b, h, G):
            m_codes, m_planes = m_mx[b]
            rows = slice(G * P, (G + 1) * P)
            nc.tensor.matmul_mx(
                out=y_banks[b][h][:],
                lhsT=m_codes[:, rows].bitcast(FP8X4),
                lhsT_scale=m_planes[:, rows],
                rhs=w_codes[:, G, h * PACK * BANK : (h + 1) * PACK * BANK].bitcast(FP8X4),
                rhs_scale=w_planes[:, G, h * BANK : (h + 1) * BANK],
                start=(G == 0),
                stop=(G == PASSES - 1),
            )

        def open_y(b):
            y_low = psum_y.tile([P, BANK], F32, name="y_low")
            y_high = psum_y.tile([P, BANK], F32, name="y_high")
            y_banks[b] = (y_low, y_high)

        def folded_pass(b, G):
            m_codes, m_planes = m_mx[b]
            if G == 0:
                folded = psum_lap.tile([P, P], F32, name="lap_t_1")
                folded_sums[b] = folded
            rows = slice(G * P, (G + 1) * P)
            for j in range(FOLDS):
                nc.tensor.matmul_mx(
                    out=folded_sums[b][:],
                    lhsT=m_codes[:, rows].bitcast(FP8X4),
                    lhsT_scale=m_planes[:, rows],
                    rhs=w_codes[:, G, j * PACK * P : (j + 1) * PACK * P].bitcast(FP8X4),
                    rhs_scale=w_planes[:, G, j * P : (j + 1) * P],
                    start=(G == 0 and j == 0),
                    stop=(G == PASSES - 1 and j == FOLDS - 1),
                )

        def mean_of_folded(b):
            unread = scrap.tile([P, P], BF16)
            negative_mean = ahead.tile([P, 1], F32)
            nc.scalar.activation(
                out=unread[:], in_=folded_sums[b][:], func=ACT.Identity,
                scale=-1.0 / FEATURES, accum_out=negative_mean[:],
            )
            neg_mean[b] = negative_mean

        def second_product(b):
            if b not in range(BLOCKS):
                return
            if b in FOLDED:
                for G in range(PASSES):
                    folded_pass(b, G)
            open_y(b)
            for h in range(HALVES):
                for G in range(PASSES):
                    second_pass(b, h, G)

        def mean_of_rows(b, h):
            if b not in range(BLOCKS):
                return
            unread = scrap.tile([P, BANK], BF16)
            if h == 0:
                low_share = ahead.tile([P, 1], F32)
                nc.scalar.activation(
                    out=unread[:], in_=y_banks[b][0][:], func=ACT.Identity,
                    scale=-1.0 / (FEATURES * BANK), accum_out=low_share[:],
                )
                low_shares[b] = low_share
            else:
                negative_mean = ahead.tile([P, 1], F32)
                nc.scalar.activation(
                    out=unread[:], in_=y_banks[b][1][:], func=ACT.Identity,
                    scale=-1.0 / FEATURES, bias=low_shares[b][:], accum_out=negative_mean[:],
                )
                neg_mean[b] = negative_mean

        def variance_of_rows(b):
            if b not in range(BLOCKS):
                return
            squares = ahead.tile([P, HALVES], F32)
            for h in range(HALVES):
                unread = scrap.tile([P, BANK], BF16)
                nc.scalar.activation(
                    out=unread[:], in_=y_banks[b][h][:], func=ACT.Square,
                    bias=neg_mean[b][:], accum_out=squares[:, h : h + 1],
                )
            low_share = ahead.tile([P, 1], F32, name="variance_share")
            nc.scalar.activation(
                out=low_share[:], in_=squares[:, 0:1], func=ACT.Identity, scale=1.0 / FEATURES, bias=EPS
            )
            variance_parts[b] = (squares, low_share)

        def inverse_std_of_rows(b):
            if b not in variance_parts:
                return
            squares, low_share = variance_parts[b]
            inverse_std = ahead.tile([P, 1], F32, name="inverse_std_scalar")
            nc.scalar.activation(
                out=inverse_std[:], in_=squares[:, 1:2], func=ACT.Abs_reciprocal_sqrt,
                scale=(1.0 / FEATURES if low_share is not None else 1.0),
                bias=(low_share[:] if low_share is not None else EPS),
            )
            inv_std[b] = inverse_std

        bank_statistics = {}

        def statistics_of_banks(b):
            partial = ahead.tile([P, HALVES, 6], F32)
            for h in range(HALVES):
                nc.vector.bn_stats(out=partial[:, h, :], in_=y_banks[b][h][:])
            bank_statistics[b] = partial

        def statistics_of_rows(b):
            partial = bank_statistics[b]
            mean_var = ahead.tile([P, 2], F32)
            nc.vector.bn_aggr(out=mean_var[:], in_=partial[:].rearrange("p h s -> p (h s)"))
            mean[b] = mean_var
            variance_parts[b] = (mean_var, None)

        def centre_half(b, h):
            if b not in range(BLOCKS):
                return
            if h == 0:
                scaled = ahead.tile([P, FEATURES], F32)
                centred[b] = scaled
            columns = slice(h * BANK, (h + 1) * BANK)
            if b in mean:
                nc.vector.scalar_tensor_tensor(
                    out=centred[b][:, columns], in0=y_banks[b][h][:], scalar=mean[b][:, 0:1],
                    in1=gamma_all[:, columns], op0=ALU.subtract, op1=ALU.mult,
                )
            else:
                nc.vector.scalar_tensor_tensor(
                    out=centred[b][:, columns], in0=y_banks[b][h][:], scalar=neg_mean[b][:],
                    in1=gamma_all[:, columns], op0=ALU.add, op1=ALU.mult,
                )

        def centre_times_gamma(b):
            centre_half(b, 0)
            centre_half(b, 1)

        beta_source = [beta_all]
        beta_banks = []

        def beta_to_psum():
            bank = psum_lap.tile([P, FEATURES], BF16, name="lap_t_0")
            for h in range(HALVES):
                columns = slice(h * BANK, (h + 1) * BANK)
                nc.tensor.matmul(
                    out=bank[:, columns], lhsT=identity_bf16[:], rhs=beta_all[:, columns], start=True, stop=True
                )
            beta_banks.append(bank)

        def normalise(b, pieces=1):
            if b not in range(BLOCKS):
                return
            z = stage.tile([P, FEATURES], F32)
            normalised[b] = z
            width = FEATURES // pieces
            for piece in range(pieces):
                columns = slice(piece * width, (piece + 1) * width)
                nc.vector.scalar_tensor_tensor(
                    out=z[:, columns], in0=centred[b][:, columns], scalar=inv_std[b][:], in1=beta_source[0][:, columns],
                    op0=ALU.mult, op1=ALU.add,
                )

        def negative_part(b):
            part = ahead.tile([P, FEATURES - SHARED_FROM], F32)
            nc.scalar.activation(
                out=part[:], in_=normalised[b][:, SHARED_FROM:], func=ACT.Relu, scale=SLOPE - 1.0
            )
            negative_parts[b] = part

        def leaky_shared(b):
            z = normalised[b]
            result = ahead.tile([P, FEATURES], F32, name="result")
            nc.gpsimd.tensor_tensor(
                out=result[:, SHARED_FROM:], in0=z[:, SHARED_FROM:], in1=negative_parts[b][:], op=ALU.add
            )
            nc.vector.scalar_tensor_tensor(
                out=result[:, 0:SHARED_FROM], in0=z[:, 0:SHARED_FROM], scalar=SLOPE, in1=z[:, 0:SHARED_FROM],
                op0=ALU.mult, op1=ALU.max,
            )
            for columns in (slice(0, SHARED_FROM), slice(SHARED_FROM, FEATURES)):
                nc.sync.dma_start(out=out_rows[:, b, columns], in_=result[:, columns])

        def leaky_and_store(b, pieces=1):
            if b not in range(BLOCKS):
                return
            z = normalised[b]
            result = ahead.tile([P, FEATURES], F32, name="result")
            width = FEATURES // pieces
            for piece in range(pieces):
                columns = slice(piece * width, (piece + 1) * width)
                nc.vector.scalar_tensor_tensor(
                    out=result[:, columns], in0=z[:, columns], scalar=SLOPE, in1=z[:, columns],
                    op0=ALU.mult, op1=ALU.max,
                )
                nc.sync.dma_start(out=out_rows[:, b, columns], in_=result[:, columns])

        feat_grouped = keep.tile([P, PASSES, PASSES, PACK, P, PACK], BF16, align_bytes=64)
        feat_codes = keep.tile([P, PASSES, PASSES, PACK, P], U32, align_bytes=64)
        feat_planes = keep.tile([P, PASSES, PASSES, PACK, P], U8, align_bytes=64)

        def regroup_feat(G, g):
            source = feat_raw[(G, g)][:].rearrange("p t (c T) -> p c t T", T=PACK)
            target = feat_grouped[:, g, G, :, :, :].rearrange("p T c t -> p c t T")
            half = 72
            nc.vector.tensor_copy(out=target[:, 0:half, :, :], in_=source[:, 0:half, :, :])
            nc.scalar.copy(out=target[:, half:P, :, :], in_=source[:, half:P, :, :])

        def quantise_feat(G, g):
            nc.vector.quantize_mx(
                out=feat_codes[:, g, G, :, :].rearrange("p T c -> p (T c)").bitcast(FP8X4),
                scales=feat_planes[:, g, G, :, :].rearrange("p T c -> p (T c)"),
                in_=feat_grouped[:, g, G, :, :, :].rearrange("p T c t -> p (T c t)"),
            )

        transpose_lap(0)
        copy_lap(0)
        regroup_feat(0, 0)
        quantise_lap(0)
        regroup_feat(0, 1)
        quantise_feat(0, 0)
        regroup_feat(1, 0)
        quantise_feat(0, 1)
        first_product(0, 0)
        regroup_feat(1, 1)
        quantise_feat(1, 0)
        transpose_lap(1)
        transpose_lap(2)
        quantise_feat(1, 1)
        round_m(0, 0)
        first_product(0, 1)
        quantise_m(0, (0,))
        copy_lap(1)
        open_y(0)
        second_pass(0, 0, 0)
        second_pass(0, 1, 0)
        round_m(0, 1)
        quantise_lap(1)
        first_product(1, 0)
        quantise_m(0, (1,))
        first_product(1, 1)
        second_pass(0, 0, 1)
        second_pass(0, 1, 1)
        copy_lap(2)
        quantise_lap(2)
        round_m(1, 0)
        first_product(2, 0)
        round_m(1, 1)
        transpose_lap(3)
        first_product(2, 1)
        copy_lap(3)
        statistics_of_banks(0)
        quantise_m(1)
        statistics_of_rows(0)
        second_product(1)
        centre_times_gamma(0)
        quantise_lap(3)
        transpose_lap(4)
        for step in range(1, BLOCKS + 1):
            late = step + 3 >= BLOCKS
            shared = late and step < BLOCKS
            if step in FOLDED:
                round_m(step + 1, 0)
                first_product(step + 2, 0)
                if step + 3 <= BLOCKS:
                    inverse_std_of_rows(step - 1)
                round_m(step + 1, 1)
                first_product(step + 2, 1)
                if shared:
                    normalise(step - 1, 2)
                mean_of_folded(step)
                copy_lap(step + 3)
            elif step + 3 < BLOCKS:
                round_m(step + 1, 0)
                first_product(step + 2, 0)
                inverse_std_of_rows(step - 1)
                mean_of_rows(step, 0)
                round_m(step + 1, 1)
                first_product(step + 2, 1)
                if step + 4 == BLOCKS:
                    beta_to_psum()
                mean_of_rows(step, 1)
                copy_lap(step + 3)
            variance_of_rows(step)
            if shared:
                negative_part(step - 1)
                inverse_std_of_rows(step)
            if not shared:
                normalise(step - 1, 2 if step == BLOCKS else 1)
            if step + 1 in FOLDED:
                transpose_lap(step + 4)
            quantise_m(step + 1)
            second_product(step + 1)
            if not late:
                leaky_and_store(step - 1)
                centre_times_gamma(step)
                quantise_lap(step + 3)
            elif shared:
                leaky_shared(step - 1)
                centre_times_gamma(step)
            else:
                leaky_and_store(step - 1, 4)
            if not (step + 1 in FOLDED):
                transpose_lap(step + 4)
            if step + 4 == BLOCKS:
                beta_source[0] = beta_banks[0]
